import numpy as np
import ml_dtypes


def mxq(x, axis, fmt="e4m3"):
    dtype, down = {"e4m3": (ml_dtypes.float8_e4m3fn, 7), "e5m2": (ml_dtypes.float8_e5m2, 14)}[fmt]
    v = np.moveaxis(np.asarray(x, np.float32).astype(ml_dtypes.bfloat16).astype(np.float64), axis, -1)
    blocks = v.reshape(v.shape[:-1] + (-1, 32))
    amax = np.abs(blocks).max(-1, keepdims=True)
    byte = np.maximum(np.where(amax > 0, np.frexp(amax)[1] - 1 + 127, 0) - down, 1)
    scale = np.exp2(byte - 127.0)
    codes = (blocks / scale).astype(np.float32).astype(dtype).astype(np.float64)
    return np.moveaxis((codes * scale).reshape(v.shape), -1, axis)


WIDE = False


def mx_kscale(k):
    if not WIDE:
        return np.ones(k)
    levels = np.array([10, -10, 5, -5, 0])
    if k % 512:
        return np.exp2(np.random.permutation(np.resize(levels, k // 32))).repeat(32)
    a = np.empty((k // 512, 16))
    for p in range(k // 512):
        a[p, :8] = np.random.permutation(np.resize(levels, 8))
        for g in range(8):
            far = levels[np.abs(levels - a[p, g]) >= 10]
            a[p, g + 8] = far[np.random.randint(len(far))]
    return np.exp2(a.ravel()).repeat(32)


BF16 = ml_dtypes.bfloat16


def bf(x):
    return np.asarray(x, np.float32).astype(BF16)


def f64(x):
    return np.asarray(x).astype(np.float64)


I, M, O, B = 512, 512, 512, 4096


def sigmoid(v):
    return 1.0 / (1.0 + np.exp(-v))


def setup_inputs():
    s, u, t = mx_kscale(I), mx_kscale(O), mx_kscale(M)
    return {
        "x": bf(np.random.standard_normal((I, B)) * s[:, None]),
        "out0": bf(np.tanh(np.random.standard_normal((O, B))) * u[:, None]),
        "mem0": bf(np.random.standard_normal((M, B)) * 0.8 * t[:, None]),
        "w_inp": bf(np.random.standard_normal((M, I)) / np.sqrt(I) / s),
        "w_rec_inp": bf(np.random.standard_normal((M, O)) / np.sqrt(O) / u),
        "w_inpgate": bf(np.random.standard_normal((M, I)) / np.sqrt(I) / s),
        "w_mem_inpgate": bf(np.random.standard_normal((M, M)) / np.sqrt(M) / t),
        "w_rec_inpgate": bf(np.random.standard_normal((M, O)) / np.sqrt(O) / u),
    }


def reference(x, out0, mem0, w_inp, w_rec_inp, w_inpgate, w_mem_inpgate, w_rec_inpgate):
    xq = mxq(f64(x), 0, "e4m3")
    oq = mxq(f64(out0), 0, "e4m3")
    mq = mxq(f64(mem0), 0, "e4m3")
    block_inp = sigmoid((mxq(f64(w_inp), 1, "e4m3") @ xq) + (mxq(f64(w_rec_inp), 1, "e4m3") @ oq))
    inp_gate = sigmoid((mxq(f64(w_inpgate), 1, "e4m3") @ xq) + (mxq(f64(w_mem_inpgate), 1, "e4m3") @ mq) + (mxq(f64(w_rec_inpgate), 1, "e4m3") @ oq))
    return block_inp * inp_gate

@@ -1,0 +1,300 @@
+from contextlib import ExitStack
+
+import concourse.mybir as mybir
+from concourse.masks import make_identity
+
+F32 = mybir.dt.float32
+BF16 = mybir.dt.bfloat16
+U32 = mybir.dt.uint32
+U8 = mybir.dt.uint8
+FP8X4 = mybir.dt.float8_e4m3fn_x4
+SIGMOID = mybir.ActivationFunctionType.Sigmoid
+MULT = mybir.AluOpType.mult
+
+P = 128
+K = 512
+M = 512
+B = 4096
+NB = 512
+NCH = B // NB
+MT = M // P
+FLOPS = 2 * 5 * M * K * B
+
+MANUAL = True
+RAW_BUFS = 3
+GRP_BUFS = 2
+CODE_BUFS = 3
+SA_BUFS = 5
+SB_BUFS = 3
+HEAD_SHARE = 128
+M_SHARE = [0,0,448,448,512,512,448,448]
+PIECES = [1,1,1,1,1,2,2,4]
+RS_AT = 0
+BANKS = [2, 3, 0, 1, 4, 5, 6, 7]
+GATE0_BANKS = [2, 3, 0, 1]
+
+
+def tile_pt_grumb_pa_t_kernel(
+    tc, x, out0, mem0, w_inp, w_rec_inp, w_inpgate, w_mem_inpgate, w_rec_inpgate, out
+):
+    nc = tc.nc
+    acts = [x, out0, mem0]
+    weights = [w_inp, w_rec_inp, w_inpgate, w_rec_inpgate, w_mem_inpgate]
+    out_view = out.rearrange("(p t) b -> p t b", t=MT)
+
+    with ExitStack() as ctx:
+        sb = ctx.enter_context(tc.tile_pool(name="sb", bufs=1))
+        ps = ctx.enter_context(tc.psum_pool(name="ps", bufs=1))
+        if MANUAL:
+            ctx.enter_context(tc.manual_schedule())
+
+        ident = sb.tile([P, P], F32, name="ident")
+        make_identity(nc, ident[:])
+        warm_in = sb.tile([P, 1], F32, name="warm_in")
+        warm_out = sb.tile([P, 1], F32, name="warm_out")
+        nc.vector.memset(warm_in[:], 0.0)
+        nc.scalar.activation(out=warm_out[:], in_=warm_in[:], func=SIGMOID)
+
+        w_raw = [sb.tile([P, MT * K], BF16, name="w_raw%d" % i) for i in range(5)]
+        w_codes = sb.tile([P, 5 * M], U32, name="w_codes", align_bytes=64)
+        w_scales = sb.tile([P, 5 * M], U8, name="w_scales", align_bytes=64)
+        w_banks = {}
+        w_grp = {}
+        raw = {}
+        grp = {}
+        codes = {}
+        scales = {}
+        sig_a = {}
+        sig_b = {}
+        acc = {}
+
+        def load_w(i):
+            nc.sync.dma_start(out=w_raw[i][:], in_=weights[i].rearrange("(p t) k -> p (t k)", t=MT))
+
+        def raw_view(op, c):
+            if c < 2:
+                if (op, c) not in raw:
+                    raw[(op, c)] = sb.tile([P, 4, NB], BF16, name="raw_h%d_%d" % (op, c))
+                return raw[(op, c)][:]
+            if op == 2:
+                if (2, c) not in raw:
+                    raw[(2, c)] = sb.tile([P, 4, NB], BF16, tag="raw_m", bufs=RAW_BUFS, name="raw_m%d" % c)
+                return raw[(2, c)][:]
+            if (0, c) not in raw:
+                raw[(0, c)] = sb.tile([P, 4, 2, NB], BF16, tag="raw_xo", bufs=RAW_BUFS, name="raw_xo%d" % c)
+            return raw[(0, c)][:, :, op, :]
+
+        def load_act(op, c):
+            nc.sync.dma_start(
+                out=raw_view(op, c),
+                in_=acts[op].rearrange("(p t) b -> p t b", t=4)[:, :, c * NB : (c + 1) * NB],
+            )
+
+        def load_chunk(c):
+            if c < NCH:
+                for op in range(3):
+                    load_act(op, c)
+
+        def transposes(i, b0):
+            words = w_raw[i][:].bitcast(F32)
+            for h in range(2):
+                bank = ps.tile([P, 4, P], F32, tag="bank%d" % (b0 + h), name="wt%d_%d" % (i, h))
+                w_banks[(i, h)] = bank
+                for j in range(4):
+                    row = 256 * (2 * h + j // 2)
+                    nc.tensor.transpose(bank[:, j, :], words[:, row + j % 2 : row + 256 : 2], ident[:])
+
+        def copy_w(i, h):
+            if h == 0:
+                w_grp[i] = sb.tile([P, MT * K], BF16, tag="w_grp", bufs=2, name="w_grp%d" % i, align_bytes=64)
+            dst = w_grp[i][:].bitcast(F32)[:, 512 * h : 512 * h + 512].rearrange("p (t m u) -> p t m u", t=2, u=2)
+            src = w_banks[(i, h)][:].rearrange("p (t u) m -> p t m u", u=2)
+            nc.scalar.copy(out=dst, in_=src)
+
+        def quant_w(i):
+            nc.vector.quantize_mx(
+                out=w_codes[:, M * i : M * i + M].bitcast(FP8X4),
+                scales=w_scales[:, M * i : M * i + M],
+                in_=w_grp[i][:],
+            )
+
+        def regroup(eng, c, src_rows, col0, w0, w1):
+            if w1 <= w0:
+                return
+            if c not in grp:
+                grp[c] = sb.tile([P, 3 * 4 * NB], BF16, tag="grp", bufs=GRP_BUFS, name="grp%d" % c, align_bytes=64)
+            dst = grp[c][:, 4 * (col0 + w0) : 4 * (col0 + w1)].rearrange("p (c i t) -> p c t i", i=4, t=4)
+            src = src_rows[:, :, w0:w1].rearrange("p t (c i) -> p c t i", i=4)
+            if eng == "V":
+                nc.vector.tensor_copy(out=dst, in_=src)
+            else:
+                nc.scalar.copy(out=dst, in_=src)
+
+        def regroup_head(c, op):
+            regroup("S", c, raw_view(op, c), op * NB, NB - HEAD_SHARE, NB)
+            regroup("V", c, raw_view(op, c), op * NB, 0, NB - HEAD_SHARE)
+
+        def regroup_v(c):
+            regroup("V", c, raw[(0, c)][:].rearrange("p t a w -> p t (a w)"), 0, 0, 2 * NB)
+            regroup("V", c, raw_view(2, c), 2 * NB, 0, NB - M_SHARE[c])
+
+        def regroup_s(c):
+            regroup("S", c, raw_view(2, c), 2 * NB, NB - M_SHARE[c], NB)
+
+        def quant(c, op0, op1):
+            if c not in codes:
+                codes[c] = sb.tile([P, 3 * NB], U32, tag="codes", bufs=CODE_BUFS, name="codes%d" % c, align_bytes=64)
+                scales[c] = sb.tile([P, 3 * NB], U8, tag="scales", bufs=CODE_BUFS, name="scales%d" % c, align_bytes=64)
+            nc.vector.quantize_mx(
+                out=codes[c][:, op0 * NB : op1 * NB].bitcast(FP8X4),
+                scales=scales[c][:, op0 * NB : op1 * NB],
+                in_=grp[c][:, op0 * 4 * NB : op1 * 4 * NB],
+            )
+
+        def quant_chunk(c):
+            quant(c, 0, 2)
+            quant(c, 2, 3)
+
+        def mx(i, c, op, t, kind, bank, start, stop, n0=0, n1=NB):
+            key = (c, kind, t, n0)
+            if start:
+                acc[key] = ps.tile([P, n1 - n0], F32, tag="bank%d" % bank, name="acc%d%s%d_%d" % (c, kind, t, n0))
+            col = M * i + P * t
+            nc.tensor.matmul_mx(
+                out=acc[key][:],
+                lhsT=w_codes[:, col : col + P].bitcast(FP8X4),
+                lhsT_scale=w_scales[:, col : col + P],
+                rhs=codes[c][:, op * NB + n0 : op * NB + n1].bitcast(FP8X4),
+                rhs_scale=scales[c][:, op * NB + n0 : op * NB + n1],
+                start=start,
+                stop=stop,
+            )
+
+        def sigmoid(c, kind, t, n0=0, n1=NB):
+            dest = sig_a if kind == "a" else sig_b
+            if c not in dest:
+                dest[c] = sb.tile(
+                    [P, MT, NB], F32, tag="sig_" + kind, bufs=SA_BUFS if kind == "a" else SB_BUFS, name="sig_%s%d" % (kind, c)
+                )
+            nc.scalar.activation(out=dest[c][:, t, n0:n1], in_=acc[(c, kind, t, n0)][:], func=SIGMOID)
+
+        def inp(c, t, bank, n0=0, n1=NB):
+            mx(0, c, 0, t, "a", bank, True, False, n0, n1)
+            mx(1, c, 1, t, "a", bank, False, True, n0, n1)
+            sigmoid(c, "a", t, n0, n1)
+
+        def gate(c, t, bank, n0=0, n1=NB):
+            mx(2, c, 0, t, "b", bank, True, False, n0, n1)
+            mx(3, c, 1, t, "b", bank, False, False, n0, n1)
+            mx(4, c, 2, t, "b", bank, False, True, n0, n1)
+            sigmoid(c, "b", t, n0, n1)
+
+        def product_store(c, t0, t1, n0=0, n1=NB):
+            nc.vector.tensor_tensor(
+                out=sig_a[c][:, t0:t1, n0:n1], in0=sig_a[c][:, t0:t1, n0:n1], in1=sig_b[c][:, t0:t1, n0:n1], op=MULT
+            )
+            nc.sync.dma_start(out=out_view[:, t0:t1, c * NB + n0 : c * NB + n1], in_=sig_a[c][:, t0:t1, n0:n1])
+
+        def finish(c):
+            step = MT // PIECES[c]
+            for t0 in range(0, MT, step):
+                product_store(c, t0, t0 + step)
+
+        load_w(0)
+        load_act(0, 0)
+        load_w(1)
+        load_act(1, 0)
+        load_w(2)
+        load_act(0, 1)
+        load_w(3)
+        load_act(1, 1)
+        load_w(4)
+        load_act(2, 0)
+        load_act(2, 1)
+        for c in range(2, 2 + RAW_BUFS):
+            load_chunk(c)
+
+        transposes(0, 0)
+        copy_w(0, 0)
+        copy_w(0, 1)
+        regroup_head(0, 0)
+        quant_w(0)
+        quant(0, 0, 1)
+        transposes(1, 2)
+        copy_w(1, 0)
+        copy_w(1, 1)
+        for t in range(MT):
+            mx(0, 0, 0, t, "a", 4 + t, True, False)
+        regroup_head(0, 1)
+        quant_w(1)
+        quant(0, 1, 2)
+        transposes(2, 0)
+        copy_w(2, 0)
+        copy_w(2, 1)
+        for t in range(MT):
+            mx(1, 0, 1, t, "a", 4 + t, False, True)
+        regroup_head(1, 0)
+        quant_w(2)
+        quant(1, 0, 1)
+        for t in range(MT):
+            sigmoid(0, "a", t)
+        transposes(3, 2)
+        copy_w(3, 0)
+        copy_w(3, 1)
+        for t in range(MT):
+            mx(0, 1, 0, t, "a", 4 + t, True, False)
+        regroup_head(1, 1)
+        quant_w(3)
+        quant(1, 1, 2)
+        transposes(4, 0)
+        copy_w(4, 0)
+        copy_w(4, 1)
+        for t in range(MT):
+            mx(1, 1, 1, t, "a", 4 + t, False, True)
+        regroup_head(0, 2)
+        quant_w(4)
+        regroup_head(1, 2)
+        quant(0, 2, 3)
+        quant(1, 2, 3)
+
+        for t in range(MT):
+            sigmoid(1, "a", t)
+        regroup_v(2)
+        gate(0, 0, GATE0_BANKS[0])
+        regroup_s(2)
+        load_chunk(2 + RAW_BUFS)
+        for t in range(1, MT):
+            gate(0, t, GATE0_BANKS[t])
+        quant_chunk(2)
+        regroup_v(3)
+        gate(1, 0, 4)
+        regroup_s(3)
+        load_chunk(3 + RAW_BUFS)
+        for t in range(1, MT):
+            gate(1, t, 4 + t)
+        finish(0)
+
+        for c in range(2, NCH):
+            ca = c + 2
+            if c + 1 < NCH:
+                quant_chunk(c + 1)
+            if ca < NCH:
+                regroup_v(ca)
+            finish(c - 1)
+            last = c == NCH - 1
+            for t in range(MT):
+                if last and t == MT - 1:
+                    for half in range(2):
+                        n0 = half * (NB // 2)
+                        n1 = n0 + NB // 2
+                        inp(c, t, BANKS[(2 * t + 2 * half) % 8], n0, n1)
+                        gate(c, t, BANKS[(2 * t + 2 * half + 1) % 8], n0, n1)
+                        product_store(c, t, t + 1, n0, n1)
+                else:
+                    inp(c, t, BANKS[2 * t])
+                    gate(c, t, BANKS[2 * t + 1])
+                    if last:
+                        product_store(c, t, t + 1)
+                if ca < NCH and t == RS_AT:
+                    regroup_s(ca)
+            load_chunk(ca + RAW_BUFS)

@@ -123,8 +123,8 @@ def tile_pt_grumb_pa_t_kernel(
                 return
             if c not in grp:
                 grp[c] = sb.tile([P, 3 * 4 * NB], BF16, tag="grp", bufs=GRP_BUFS, name="grp%d" % c, align_bytes=64)
-            dst = grp[c][:, 4 * (col0 + w0) : 4 * (col0 + w1)].rearrange("p (c i t) -> p c t i", i=4, t=4)
-            src = src_rows[:, :, w0:w1].rearrange("p t (c i) -> p c t i", i=4)
+            dst = grp[c][:, 4 * (col0 + w0) : 4 * (col0 + w1)].rearrange("p (c i t) -> p c t i", i=8, t=4)
+            src = src_rows[:, :, w0:w1].rearrange("p t (c i) -> p c t i", i=8)
             if eng == "V":
                 nc.vector.tensor_copy(out=dst, in_=src)
             else:

@@ -104,12 +104,15 @@ def tile_pt_grumb_pa_t_kernel(
                     row = 256 * (2 * h + j // 2)
                     nc.tensor.transpose(bank[:, j, :], words[:, row + j % 2 : row + 256 : 2], ident[:])
 
-        def copy_w(i, h):
+        def copy_w(i, h, eng="S"):
             if h == 0:
                 w_grp[i] = sb.tile([P, MT * K], BF16, tag="w_grp", bufs=2, name="w_grp%d" % i, align_bytes=64)
             dst = w_grp[i][:].bitcast(F32)[:, 512 * h : 512 * h + 512].rearrange("p (t m u) -> p t m u", t=2, u=2)
             src = w_banks[(i, h)][:].rearrange("p (t u) m -> p t m u", u=2)
-            nc.scalar.copy(out=dst, in_=src)
+            if eng == "S":
+                nc.scalar.copy(out=dst, in_=src)
+            else:
+                nc.vector.tensor_copy(out=dst, in_=src)
 
         def quant_w(i):
             nc.vector.quantize_mx(
@@ -130,8 +133,10 @@ def tile_pt_grumb_pa_t_kernel(
             else:
                 nc.scalar.copy(out=dst, in_=src)
 
-        def regroup_head(c, op):
+        def head_s(c, op):
             regroup("S", c, raw_view(op, c), op * NB, NB - HEAD_SHARE, NB)
+
+        def head_v(c, op):
             regroup("V", c, raw_view(op, c), op * NB, 0, NB - HEAD_SHARE)
 
         def regroup_v(c):
@@ -200,78 +205,84 @@ def tile_pt_grumb_pa_t_kernel(
             for t0 in range(0, MT, step):
                 product_store(c, t0, t0 + step)
 
-        load_w(0)
         load_act(0, 0)
-        load_w(1)
+        load_w(0)
         load_act(1, 0)
-        load_w(2)
+        load_w(1)
         load_act(0, 1)
-        load_w(3)
         load_act(1, 1)
-        load_w(4)
+        load_w(2)
+        load_w(3)
         load_act(2, 0)
+        load_w(4)
         load_act(2, 1)
-        for c in range(2, 2 + RAW_BUFS):
-            load_chunk(c)
-
+        load_chunk(2)
+        load_chunk(3)
+        load_chunk(4)
+        head_s(0, 0)
+        head_v(0, 0)
+        quant(0, 0, 1)
         transposes(0, 0)
         copy_w(0, 0)
         copy_w(0, 1)
-        regroup_head(0, 0)
+        head_s(0, 1)
+        head_v(0, 1)
         quant_w(0)
-        quant(0, 0, 1)
+        quant(0, 1, 2)
         transposes(1, 2)
         copy_w(1, 0)
         copy_w(1, 1)
         for t in range(MT):
             mx(0, 0, 0, t, "a", 4 + t, True, False)
-        regroup_head(0, 1)
+        head_s(1, 0)
+        head_v(1, 0)
         quant_w(1)
-        quant(0, 1, 2)
-        transposes(2, 0)
-        copy_w(2, 0)
-        copy_w(2, 1)
-        for t in range(MT):
-            mx(1, 0, 1, t, "a", 4 + t, False, True)
-        regroup_head(1, 0)
-        quant_w(2)
         quant(1, 0, 1)
         for t in range(MT):
+            mx(1, 0, 1, t, "a", 4 + t, False, True)
+        head_s(1, 1)
+        head_v(1, 1)
+        for t in range(MT):
             sigmoid(0, "a", t)
+        transposes(2, 0)
+        copy_w(2, 0, "V")
+        copy_w(2, 1)
+        quant(1, 1, 2)
         transposes(3, 2)
         copy_w(3, 0)
         copy_w(3, 1)
+        head_s(0, 2)
+        head_v(0, 2)
+        quant_w(2)
+        quant_w(3)
+        quant(0, 2, 3)
+        transposes(4, 0)
         for t in range(MT):
             mx(0, 1, 0, t, "a", 4 + t, True, False)
-        regroup_head(1, 1)
-        quant_w(3)
-        quant(1, 1, 2)
-        transposes(4, 0)
+            mx(1, 1, 1, t, "a", 4 + t, False, True)
         copy_w(4, 0)
         copy_w(4, 1)
-        for t in range(MT):
-            mx(1, 1, 1, t, "a", 4 + t, False, True)
-        regroup_head(0, 2)
+        head_s(1, 2)
+        head_v(1, 2)
         quant_w(4)
-        regroup_head(1, 2)
-        quant(0, 2, 3)
         quant(1, 2, 3)
-
         for t in range(MT):
             sigmoid(1, "a", t)
         regroup_v(2)
-        gate(0, 0, GATE0_BANKS[0])
+        gate(0, 0, 2)
         regroup_s(2)
-        load_chunk(2 + RAW_BUFS)
-        for t in range(1, MT):
-            gate(0, t, GATE0_BANKS[t])
+        load_chunk(5)
+        gate(0, 1, 3)
+        gate(0, 2, 0)
+        gate(0, 3, 1)
         quant_chunk(2)
         regroup_v(3)
         gate(1, 0, 4)
         regroup_s(3)
-        load_chunk(3 + RAW_BUFS)
-        for t in range(1, MT):
-            gate(1, t, 4 + t)
+        load_chunk(6)
+        gate(1, 1, 5)
+        gate(1, 2, 6)
+        gate(1, 3, 7)
         finish(0)
 
         for c in range(2, NCH):

@@ -27,8 +27,8 @@ CODE_BUFS = 3
 SA_BUFS = 5
 SB_BUFS = 3
 HEAD_SHARE = 128
-M_SHARE = [0,0,448,448,512,512,448,448]
-PIECES = [1,1,1,1,1,2,2,4]
+M_SHARE = [0,0,384,512,512,512,384,512]
+PIECES = [1,1,1,1,2,4,4]
 RS_AT = 0
 BANKS = [2, 3, 0, 1, 4, 5, 6, 7]
 GATE0_BANKS = [2, 3, 0, 1]

@@ -27,7 +27,7 @@ CODE_BUFS = 3
 SA_BUFS = 5
 SB_BUFS = 3
 HEAD_SHARE = 128
-M_SHARE = [0,0,384,512,512,512,384,512]
+M_SHARE = [0,0,384,512,384,512,384,512]
 PIECES = [1,1,1,1,2,4,4]
 RS_AT = 0
 BANKS = [2, 3, 0, 1, 4, 5, 6, 7]

from contextlib import ExitStack

import concourse.mybir as mybir
from concourse.masks import make_identity

F32 = mybir.dt.float32
BF16 = mybir.dt.bfloat16
U32 = mybir.dt.uint32
U8 = mybir.dt.uint8
FP8X4 = mybir.dt.float8_e4m3fn_x4
SIGMOID = mybir.ActivationFunctionType.Sigmoid
MULT = mybir.AluOpType.mult

P = 128
K = 512
M = 512
B = 4096
NB = 512
NCH = B // NB
MT = M // P
FLOPS = 2 * 5 * M * K * B

MANUAL = True
RAW_BUFS = 3
GRP_BUFS = 2
CODE_BUFS = 3
SA_BUFS = 5
SB_BUFS = 3
HEAD_SHARE = 128
M_SHARE = [0,0,384,512,384,512,384,512]
PIECES = [1,1,1,1,2,4,4]
RS_AT = 0
BANKS = [2, 3, 0, 1, 4, 5, 6, 7]
GATE0_BANKS = [2, 3, 0, 1]


def tile_pt_grumb_pa_t_kernel(
    tc, x, out0, mem0, w_inp, w_rec_inp, w_inpgate, w_mem_inpgate, w_rec_inpgate, out
):
    nc = tc.nc
    acts = [x, out0, mem0]
    weights = [w_inp, w_rec_inp, w_inpgate, w_rec_inpgate, w_mem_inpgate]
    out_view = out.rearrange("(p t) b -> p t b", t=MT)

    with ExitStack() as ctx:
        sb = ctx.enter_context(tc.tile_pool(name="sb", bufs=1))
        ps = ctx.enter_context(tc.psum_pool(name="ps", bufs=1))
        if MANUAL:
            ctx.enter_context(tc.manual_schedule())

        ident = sb.tile([P, P], F32, name="ident")
        make_identity(nc, ident[:])
        warm_in = sb.tile([P, 1], F32, name="warm_in")
        warm_out = sb.tile([P, 1], F32, name="warm_out")
        nc.vector.memset(warm_in[:], 0.0)
        nc.scalar.activation(out=warm_out[:], in_=warm_in[:], func=SIGMOID)

        w_raw = [sb.tile([P, MT * K], BF16, name="w_raw%d" % i) for i in range(5)]
        w_codes = sb.tile([P, 5 * M], U32, name="w_codes", align_bytes=64)
        w_scales = sb.tile([P, 5 * M], U8, name="w_scales", align_bytes=64)
        w_banks = {}
        w_grp = {}
        raw = {}
        grp = {}
        codes = {}
        scales = {}
        sig_a = {}
        sig_b = {}
        acc = {}

        def load_w(i):
            nc.sync.dma_start(out=w_raw[i][:], in_=weights[i].rearrange("(p t) k -> p (t k)", t=MT))

        def raw_view(op, c):
            if c < 2:
                if (op, c) not in raw:
                    raw[(op, c)] = sb.tile([P, 4, NB], BF16, name="raw_h%d_%d" % (op, c))
                return raw[(op, c)][:]
            if op == 2:
                if (2, c) not in raw:
                    raw[(2, c)] = sb.tile([P, 4, NB], BF16, tag="raw_m", bufs=RAW_BUFS, name="raw_m%d" % c)
                return raw[(2, c)][:]
            if (0, c) not in raw:
                raw[(0, c)] = sb.tile([P, 4, 2, NB], BF16, tag="raw_xo", bufs=RAW_BUFS, name="raw_xo%d" % c)
            return raw[(0, c)][:, :, op, :]

        def load_act(op, c):
            nc.sync.dma_start(
                out=raw_view(op, c),
                in_=acts[op].rearrange("(p t) b -> p t b", t=4)[:, :, c * NB : (c + 1) * NB],
            )

        def load_chunk(c):
            if c < NCH:
                for op in range(3):
                    load_act(op, c)

        def transposes(i, b0):
            words = w_raw[i][:].bitcast(F32)
            for h in range(2):
                bank = ps.tile([P, 4, P], F32, tag="bank%d" % (b0 + h), name="wt%d_%d" % (i, h))
                w_banks[(i, h)] = bank
                for j in range(4):
                    row = 256 * (2 * h + j // 2)
                    nc.tensor.transpose(bank[:, j, :], words[:, row + j % 2 : row + 256 : 2], ident[:])

        def copy_w(i, h, eng="S"):
            if h == 0:
                w_grp[i] = sb.tile([P, MT * K], BF16, tag="w_grp", bufs=2, name="w_grp%d" % i, align_bytes=64)
            dst = w_grp[i][:].bitcast(F32)[:, 512 * h : 512 * h + 512].rearrange("p (t m u) -> p t m u", t=2, u=2)
            src = w_banks[(i, h)][:].rearrange("p (t u) m -> p t m u", u=2)
            if eng == "S":
                nc.scalar.copy(out=dst, in_=src)
            else:
                nc.vector.tensor_copy(out=dst, in_=src)

        def quant_w(i):
            nc.vector.quantize_mx(
                out=w_codes[:, M * i : M * i + M].bitcast(FP8X4),
                scales=w_scales[:, M * i : M * i + M],
                in_=w_grp[i][:],
            )

        def regroup(eng, c, src_rows, col0, w0, w1):
            if w1 <= w0:
                return
            if c not in grp:
                grp[c] = sb.tile([P, 3 * 4 * NB], BF16, tag="grp", bufs=GRP_BUFS, name="grp%d" % c, align_bytes=64)
            dst = grp[c][:, 4 * (col0 + w0) : 4 * (col0 + w1)].rearrange("p (c i t) -> p c t i", i=8, t=4)
            src = src_rows[:, :, w0:w1].rearrange("p t (c i) -> p c t i", i=8)
            if eng == "V":
                nc.vector.tensor_copy(out=dst, in_=src)
            else:
                nc.scalar.copy(out=dst, in_=src)

        def head_s(c, op):
            regroup("S", c, raw_view(op, c), op * NB, NB - HEAD_SHARE, NB)

        def head_v(c, op):
            regroup("V", c, raw_view(op, c), op * NB, 0, NB - HEAD_SHARE)

        def regroup_v(c):
            regroup("V", c, raw[(0, c)][:].rearrange("p t a w -> p t (a w)"), 0, 0, 2 * NB)
            regroup("V", c, raw_view(2, c), 2 * NB, 0, NB - M_SHARE[c])

        def regroup_s(c):
            regroup("S", c, raw_view(2, c), 2 * NB, NB - M_SHARE[c], NB)

        def quant(c, op0, op1):
            if c not in codes:
                codes[c] = sb.tile([P, 3 * NB], U32, tag="codes", bufs=CODE_BUFS, name="codes%d" % c, align_bytes=64)
                scales[c] = sb.tile([P, 3 * NB], U8, tag="scales", bufs=CODE_BUFS, name="scales%d" % c, align_bytes=64)
            nc.vector.quantize_mx(
                out=codes[c][:, op0 * NB : op1 * NB].bitcast(FP8X4),
                scales=scales[c][:, op0 * NB : op1 * NB],
                in_=grp[c][:, op0 * 4 * NB : op1 * 4 * NB],
            )

        def quant_chunk(c):
            quant(c, 0, 2)
            quant(c, 2, 3)

        def mx(i, c, op, t, kind, bank, start, stop, n0=0, n1=NB):
            key = (c, kind, t, n0)
            if start:
                acc[key] = ps.tile([P, n1 - n0], F32, tag="bank%d" % bank, name="acc%d%s%d_%d" % (c, kind, t, n0))
            col = M * i + P * t
            nc.tensor.matmul_mx(
                out=acc[key][:],
                lhsT=w_codes[:, col : col + P].bitcast(FP8X4),
                lhsT_scale=w_scales[:, col : col + P],
                rhs=codes[c][:, op * NB + n0 : op * NB + n1].bitcast(FP8X4),
                rhs_scale=scales[c][:, op * NB + n0 : op * NB + n1],
                start=start,
                stop=stop,
            )

        def sigmoid(c, kind, t, n0=0, n1=NB):
            dest = sig_a if kind == "a" else sig_b
            if c not in dest:
                dest[c] = sb.tile(
                    [P, MT, NB], F32, tag="sig_" + kind, bufs=SA_BUFS if kind == "a" else SB_BUFS, name="sig_%s%d" % (kind, c)
                )
            nc.scalar.activation(out=dest[c][:, t, n0:n1], in_=acc[(c, kind, t, n0)][:], func=SIGMOID)

        def inp(c, t, bank, n0=0, n1=NB):
            mx(0, c, 0, t, "a", bank, True, False, n0, n1)
            mx(1, c, 1, t, "a", bank, False, True, n0, n1)
            sigmoid(c, "a", t, n0, n1)

        def gate(c, t, bank, n0=0, n1=NB):
            mx(2, c, 0, t, "b", bank, True, False, n0, n1)
            mx(3, c, 1, t, "b", bank, False, False, n0, n1)
            mx(4, c, 2, t, "b", bank, False, True, n0, n1)
            sigmoid(c, "b", t, n0, n1)

        def product_store(c, t0, t1, n0=0, n1=NB):
            nc.vector.tensor_tensor(
                out=sig_a[c][:, t0:t1, n0:n1], in0=sig_a[c][:, t0:t1, n0:n1], in1=sig_b[c][:, t0:t1, n0:n1], op=MULT
            )
            nc.sync.dma_start(out=out_view[:, t0:t1, c * NB + n0 : c * NB + n1], in_=sig_a[c][:, t0:t1, n0:n1])

        def finish(c):
            step = MT // PIECES[c]
            for t0 in range(0, MT, step):
                product_store(c, t0, t0 + step)

        load_act(0, 0)
        load_w(0)
        load_act(1, 0)
        load_w(1)
        load_act(0, 1)
        load_act(1, 1)
        load_w(2)
        load_w(3)
        load_act(2, 0)
        load_w(4)
        load_act(2, 1)
        load_chunk(2)
        load_chunk(3)
        load_chunk(4)
        head_s(0, 0)
        head_v(0, 0)
        quant(0, 0, 1)
        transposes(0, 0)
        copy_w(0, 0)
        copy_w(0, 1)
        head_s(0, 1)
        head_v(0, 1)
        quant_w(0)
        quant(0, 1, 2)
        transposes(1, 2)
        copy_w(1, 0)
        copy_w(1, 1)
        for t in range(MT):
            mx(0, 0, 0, t, "a", 4 + t, True, False)
        head_s(1, 0)
        head_v(1, 0)
        quant_w(1)
        quant(1, 0, 1)
        for t in range(MT):
            mx(1, 0, 1, t, "a", 4 + t, False, True)
        head_s(1, 1)
        head_v(1, 1)
        for t in range(MT):
            sigmoid(0, "a", t)
        transposes(2, 0)
        copy_w(2, 0, "V")
        copy_w(2, 1)
        quant(1, 1, 2)
        transposes(3, 2)
        copy_w(3, 0)
        copy_w(3, 1)
        head_s(0, 2)
        head_v(0, 2)
        quant_w(2)
        quant_w(3)
        quant(0, 2, 3)
        transposes(4, 0)
        for t in range(MT):
            mx(0, 1, 0, t, "a", 4 + t, True, False)
            mx(1, 1, 1, t, "a", 4 + t, False, True)
        copy_w(4, 0)
        copy_w(4, 1)
        head_s(1, 2)
        head_v(1, 2)
        quant_w(4)
        quant(1, 2, 3)
        for t in range(MT):
            sigmoid(1, "a", t)
        regroup_v(2)
        gate(0, 0, 2)
        regroup_s(2)
        load_chunk(5)
        gate(0, 1, 3)
        gate(0, 2, 0)
        gate(0, 3, 1)
        quant_chunk(2)
        regroup_v(3)
        gate(1, 0, 4)
        regroup_s(3)
        load_chunk(6)
        gate(1, 1, 5)
        gate(1, 2, 6)
        gate(1, 3, 7)
        finish(0)

        for c in range(2, NCH):
            ca = c + 2
            if c + 1 < NCH:
                quant_chunk(c + 1)
            if ca < NCH:
                regroup_v(ca)
            finish(c - 1)
            last = c == NCH - 1
            for t in range(MT):
                if last and t == MT - 1:
                    for half in range(2):
                        n0 = half * (NB // 2)
                        n1 = n0 + NB // 2
                        inp(c, t, BANKS[(2 * t + 2 * half) % 8], n0, n1)
                        gate(c, t, BANKS[(2 * t + 2 * half + 1) % 8], n0, n1)
                        product_store(c, t, t + 1, n0, n1)
                else:
                    inp(c, t, BANKS[2 * t])
                    gate(c, t, BANKS[2 * t + 1])
                    if last:
                        product_store(c, t, t + 1)
                if ca < NCH and t == RS_AT:
                    regroup_s(ca)
            load_chunk(ca + RAW_BUFS)
